import numpy as np
import ml_dtypes


BF16 = ml_dtypes.bfloat16


def bf(x):
    return np.asarray(x, np.float32).astype(BF16)


def f64(x):
    return np.asarray(x).astype(np.float64)


E2M1 = np.array([0.0, 0.5, 1.0, 1.5, 2.0, 3.0, 4.0, 6.0, -0.0, -0.5, -1.0, -1.5, -2.0, -3.0, -4.0, -6.0])


def pack_weight(w, fmt):
    k, n = w.shape
    w = f64(bf(w)).reshape(k // 32, 32, n)
    amax = np.abs(w).max(1)
    if fmt == "e4m3":
        byte = np.frexp(amax)[1] - 1 + 127 - 7
    else:
        mant, ex = np.frexp(amax / 6.0)
        byte = np.where(mant > 0.5, ex, ex - 1) + 127
    byte = np.clip(np.where(amax > 0, byte, 1), 1, 254)
    scaled = (w * np.exp2(127.0 - byte)[:, None, :]).reshape(k, n).astype(np.float32)
    by_word = np.ascontiguousarray(scaled.reshape(k // 512, 128, 4, n).transpose(0, 1, 3, 2))
    if fmt == "e4m3":
        words = by_word.astype(ml_dtypes.float8_e4m3fn).view(np.uint8)
    else:
        c = by_word.astype(ml_dtypes.float4_e2m1fn).view(np.uint8) & 0xF
        words = c[..., 0::2] | (c[..., 1::2] << 4)
    return np.ascontiguousarray(words), np.ascontiguousarray(byte.astype(np.uint8).reshape(k // 512, 16, n))


def unpack_weight(words, scales, fmt):
    g, p, n, _ = words.shape
    if fmt == "e4m3":
        vals = np.ascontiguousarray(words).view(ml_dtypes.float8_e4m3fn).astype(np.float64)
    else:
        nib = np.empty((g, p, n, 4), np.uint8)
        nib[..., 0::2] = words & 0xF
        nib[..., 1::2] = words >> 4
        vals = E2M1[nib]
    vals = vals * np.repeat(np.exp2(scales.astype(np.float64) - 127.0), 8, axis=1)[..., None]
    return vals.transpose(0, 1, 3, 2).reshape(g * 512, n)

def pack4(w):
    words, scales = pack_weight(w, "e2m1")
    return words.reshape(words.shape[0], 128, -1), scales


def unpack4(words, scales):
    return unpack_weight(words.reshape(words.shape[0], 128, -1, 2), scales, "e2m1")


def kspread(k):
    return np.exp2(np.repeat(np.random.randint(-6, 7, k // 32), 32).astype(np.float64))


B, T, H, KV, HD = 1, 512, 16, 4, 160
D = H * HD
KVD = KV * HD
O = D + 2 * KVD
ROPE_BASE = 500000.0
CLAMP = 8.0


def rope(u):
    n = u.shape[1]
    inv = 1.0 / ROPE_BASE ** (np.arange(0, HD, 2) / HD)
    freqs = np.arange(T)[:, None] * inv[None, :]
    cos, sin = np.cos(freqs)[None, None], np.sin(freqs)[None, None]
    p = u.reshape(B, n, T, HD // 2, 2)
    a, b = p[..., 0], p[..., 1]
    return np.stack([a * cos - b * sin, a * sin + b * cos], axis=-1).reshape(B, n, T, HD)


def setup_inputs():
    s = kspread(D)
    x = np.random.standard_normal((B, T, D)) * s
    x_words, x_scales = pack4(np.ascontiguousarray(x.reshape(B * T, D).T))
    w = np.random.standard_normal((O, D)) * 0.5 * CLAMP / np.sqrt(D) / s[None, :]
    words, scales = pack4(np.ascontiguousarray(w.T))
    return {"x_words": x_words, "x_scales": x_scales, "w_qkv_words": words, "w_qkv_scales": scales}


def reference(x_words, x_scales, w_qkv_words, w_qkv_scales):
    qkv = unpack4(x_words, x_scales).T.reshape(B, T, D) @ unpack4(w_qkv_words, w_qkv_scales)
    q = qkv[..., :D].reshape(B, T, H, HD).transpose(0, 2, 1, 3)
    k = qkv[..., D:D + KVD].reshape(B, T, KV, HD).transpose(0, 2, 1, 3)
    v = qkv[..., D + KVD:].reshape(B, T, KV, HD).transpose(0, 2, 1, 3)
    q = np.clip(rope(q), -CLAMP, CLAMP)
    k = np.clip(rope(k), -CLAMP, CLAMP)
    v = np.clip(v, -CLAMP, CLAMP)
    return q, k, v

@@ -1,0 +1,226 @@
+import math
+from contextlib import ExitStack
+
+import concourse.mybir as mybir
+
+F32 = mybir.dt.float32
+I32 = mybir.dt.int32
+U8 = mybir.dt.uint8
+FP4X4 = mybir.dt.float4_e2m1fn_x4
+ALU = mybir.AluOpType
+ACT = mybir.ActivationFunctionType
+
+P = 128
+T, H, KV, HD = 512, 16, 4, 160
+D = H * HD
+KVD = KV * HD
+O = D + 2 * KVD
+K = D
+PASSES = K // 512
+M_TILES = T // P
+ROPE_BASE = 500000.0
+CLAMP = 8.0
+
+FLOPS = 2 * T * K * O
+BYTES = K * T // 2 + K * T // 32 + K * O // 2 + K * O // 32 + 4 * T * O
+
+LOADS = [(0, 512), (512, 512), (1024, 1024), (2048, 1024), (3072, 768)]
+BLOCKS = [(0, 512), (512, 512), (1024, 512), (1536, 512), (2048, 512), (2560, 512), (3072, 256), (3328, 512)]
+GPSIMD_CLIPS = (2, 6, 10, 14, 18, 22)
+REPEAT = 4
+TABLE = REPEAT * HD
+
+
+def tile_dbrxattention_pa_kernel(tc, x_words, x_scales, w_words, w_scales, out_q, out_k, out_v):
+    nc = tc.nc
+    with ExitStack() as ctx:
+        keep = ctx.enter_context(tc.tile_pool(name="keep", bufs=1))
+        work = ctx.enter_context(tc.tile_pool(name="work", bufs=4))
+        psum = ctx.enter_context(tc.psum_pool(name="psum", bufs=8))
+        ctx.enter_context(tc.manual_schedule())
+
+        xw = keep.tile([P, PASSES, 2 * T], U8, name="xw", align_bytes=64)
+        xs = keep.tile([P, PASSES, T], U8, name="xs", align_bytes=64)
+        ww = [keep.tile([P, PASSES, 2 * n], U8, name="ww%d" % i, align_bytes=64) for i, (c, n) in enumerate(LOADS)]
+        ws = [keep.tile([P, PASSES, n], U8, name="ws%d" % i, align_bytes=64) for i, (c, n) in enumerate(LOADS)]
+
+        def zero(engine, plane):
+            engine.memset(plane[:].rearrange("p g n -> p (g n)").bitcast(I32), 0)
+
+        def load_words(dst, src, g0, g1):
+            nc.sync.dma_start(
+                out=dst[:, g0:g1, :].bitcast(I32),
+                in_=src[g0:g1].rearrange("g p n -> p g n").bitcast(I32),
+            )
+
+        def load_scales(dst, src):
+            for quad in range(4):
+                nc.sync.dma_start(
+                    out=dst[32 * quad : 32 * quad + 4, :, :].bitcast(I32),
+                    in_=src[:, 4 * quad : 4 * quad + 4, :].rearrange("g r n -> r g n").bitcast(I32),
+                )
+
+        def w_cols(i):
+            c, n = LOADS[i]
+            return w_words[:, :, 2 * c : 2 * (c + n)]
+
+        def s_cols(i):
+            c, n = LOADS[i]
+            return w_scales[:, :, c : c + n]
+
+        pos = keep.tile([P, M_TILES], F32, name="pos")
+        nc.gpsimd.iota(pos[:], pattern=[[P, M_TILES]], base=0, channel_multiplier=1,
+                       allow_small_or_imprecise_dtypes=True)
+        zero(nc.vector, xs)
+        zero(nc.vector, ws[0])
+        for i in range(1, len(LOADS)):
+            zero(nc.gpsimd, ws[i])
+
+        load_words(xw, x_words, 0, 1)
+        load_words(ww[0], w_cols(0), 0, 1)
+        load_scales(xs, x_scales)
+        load_scales(ws[0], s_cols(0))
+        load_words(xw, x_words, 1, 3)
+        load_words(ww[0], w_cols(0), 1, 3)
+        load_words(xw, x_words, 3, 5)
+        load_words(ww[0], w_cols(0), 3, 5)
+        for i in range(1, len(LOADS)):
+            load_words(ww[i], w_cols(i), 0, PASSES)
+            load_scales(ws[i], s_cols(i))
+
+        ratio = ROPE_BASE ** (-2.0 / HD)
+        inv = keep.tile([P, HD], F32, name="inv")
+        nc.vector.memset(inv[:, 0:1], -1.0)
+        nc.vector.memset(inv[:, 1:2], 1.0)
+        width = 2
+        while width < HD:
+            more = min(width, HD - width)
+            nc.vector.tensor_scalar_mul(inv[:, width : width + more], inv[:, 0:more], ratio ** (width // 2))
+            width += more
+
+        sin_t = [keep.tile([P, TABLE], F32, name="sin%d" % m) for m in range(M_TILES)]
+        cos_t = [keep.tile([P, TABLE], F32, name="cos%d" % m) for m in range(M_TILES)]
+
+        def angles(m0, m1, name):
+            count = m1 - m0
+            turns = keep.tile([P, 2, count, HD], F32, name="turns" + name)
+            whole = keep.tile([P, 2, count, HD], I32, name="whole" + name)
+            for m in range(m0, m1):
+                nc.vector.tensor_scalar(out=turns[:, 0, m - m0, :], in0=inv[:], scalar1=pos[:, m : m + 1],
+                                        scalar2=1.0 / (2.0 * math.pi), op0=ALU.mult, op1=ALU.mult)
+            nc.vector.tensor_scalar_add(turns[:, 1, :, :], turns[:, 0, :, :], 0.25)
+            nc.vector.tensor_copy(out=whole[:], in_=turns[:])
+            nc.vector.tensor_tensor(out=turns[:], in0=turns[:], in1=whole[:], op=ALU.subtract)
+            for m in range(m0, m1):
+                for kind, table in ((1, cos_t[m]), (0, sin_t[m])):
+                    nc.scalar.activation(
+                        out=table[:].rearrange("p (h d) -> p h d", d=HD),
+                        in_=turns[:, kind, m - m0 : m - m0 + 1, :].to_broadcast([P, REPEAT, HD]),
+                        func=ACT.Sin, scale=2.0 * math.pi)
+
+        angles(0, 1, "a")
+        angles(1, M_TILES, "b")
+
+        res_q = [keep.tile([P, D], F32, name="q%d" % m) for m in range(M_TILES)]
+        res_k = [keep.tile([P, KVD], F32, name="k%d" % m) for m in range(M_TILES)]
+        res_v = [keep.tile([P, KVD], F32, name="v%d" % m) for m in range(M_TILES)]
+
+        def one_pass(acc, m, c, n, g):
+            i = max(j for j in range(len(LOADS)) if LOADS[j][0] <= c)
+            at = c - LOADS[i][0]
+            nc.tensor.matmul_mx(
+                out=acc,
+                lhsT=xw[:, g, 2 * P * m : 2 * P * (m + 1)].bitcast(FP4X4),
+                lhsT_scale=xs[:, g, P * m : P * (m + 1)],
+                rhs=ww[i][:, g, 2 * at : 2 * (at + n)].bitcast(FP4X4),
+                rhs_scale=ws[i][:, g, at : at + n],
+                start=(g == 0), stop=(g == PASSES - 1))
+
+        turn = [0]
+        chain = []
+        ready = {}
+        stored = {}
+        results = {"q": (out_q, res_q), "k": (out_k, res_k), "v": (out_v, res_v)}
+
+        def done(which, m, c0, c1):
+            key = (which, m)
+            assert ready.get(key, 0) == c0
+            ready[key] = c1
+            h0, h1 = stored.get(key, 0), c1 // HD
+            if h1 > h0:
+                stored[key] = h1
+                dram, res = results[which]
+                nc.sync.dma_start(
+                    out=dram[0, h0:h1, P * m : P * (m + 1), :].rearrange("h p d -> p h d"),
+                    in_=res[m][:, HD * h0 : HD * h1].rearrange("p (h d) -> p h d", d=HD))
+
+        def step_chain(entry):
+            step, y, n, which, m, c0 = entry
+            if step == 0:
+                nc.scalar.activation(out=y[:, :n], in_=y[:, :n], func=ACT.Relu, scale=-1.0, bias=CLAMP)
+            elif step == 1:
+                nc.scalar.activation(out=y[:, :n], in_=y[:, :n], func=ACT.Relu, scale=-1.0, bias=2.0 * CLAMP)
+            else:
+                nc.scalar.activation(out=results[which][1][m][:, c0 : c0 + n], in_=y[:, :n], func=ACT.Identity, bias=-CLAMP)
+                done(which, m, c0, c0 + n)
+            entry[0] = step + 1
+
+        def advance(entry):
+            if entry is not None:
+                chain.append(entry)
+            for e in list(chain):
+                step_chain(e)
+            while chain and chain[0][0] == 3:
+                chain.pop(0)
+
+        def rope(acc, m, c, n, which, c0):
+            off = c % HD
+            a = work.tile([P, 512], F32, name="a")
+            b = work.tile([P, 512], F32, name="b")
+            y = work.tile([P, 512], F32, name="y", bufs=8)
+            nc.vector.tensor_tensor(out=a[:, :n], in0=acc, in1=cos_t[m][:, off : off + n], op=ALU.mult)
+            nc.vector.tensor_tensor(
+                out=b[:, :n].rearrange("p (i t) -> p i t", t=2),
+                in0=acc.rearrange("p (i t) -> p i t", t=2)[:, :, ::-1],
+                in1=sin_t[m][:, off : off + n].rearrange("p (i t) -> p i t", t=2), op=ALU.mult)
+            nc.gpsimd.tensor_tensor(out=y[:, :n], in0=a[:, :n], in1=b[:, :n], op=ALU.add)
+            if which == "k" and c0 > 0 or turn[0] in GPSIMD_CLIPS:
+                nc.gpsimd.tensor_scalar(out=results[which][1][m][:, c0 : c0 + n], in0=y[:, :n], scalar1=CLAMP, scalar2=-CLAMP, op0=ALU.min, op1=ALU.max)
+                done(which, m, c0, c0 + n)
+            else:
+                advance([0, y, n, which, m, c0])
+            turn[0] += 1
+
+        def finish(acc, m, c, n):
+            if c < D:
+                rope(acc[:, :n], m, c, n, "q", c)
+                return
+            kn = max(0, min(n, D + KVD - c))
+            if kn:
+                rope(acc[:, :kn], m, c, kn, "k", c - D)
+            if kn < n:
+                if kn == 0:
+                    advance(None)
+                v0 = c + kn - D - KVD
+                v1 = c + n - D - KVD
+                nc.vector.tensor_scalar(out=res_v[m][:, v0:v1], in0=acc[:, kn:n], scalar1=CLAMP, scalar2=-CLAMP,
+                                        op0=ALU.min, op1=ALU.max)
+                done("v", m, v0, v1)
+
+        for b, (c, n) in enumerate(BLOCKS):
+            if c == D + 512:
+                advance(None)
+                advance(None)
+            if b == 0:
+                accs = [psum.tile([P, 512], F32, name="acc") for m in range(M_TILES)]
+                for g in range(PASSES):
+                    for m in range(M_TILES):
+                        one_pass(accs[m][:, :n], m, c, n, g)
+                for m in range(M_TILES):
+                    finish(accs[m], m, c, n)
+            else:
+                for m in range(M_TILES):
+                    acc = psum.tile([P, 512], F32, name="acc")
+                    for g in range(PASSES):
+                        one_pass(acc[:, :n], m, c, n, g)
+                    finish(acc, m, c, n)

@@ -90,8 +90,8 @@ def tile_dbrxattention_pa_kernel(tc, x_words, x_scales, w_words, w_scales, out_q
 
         ratio = ROPE_BASE ** (-2.0 / HD)
         inv = keep.tile([P, HD], F32, name="inv")
-        nc.vector.memset(inv[:, 0:1], -1.0)
-        nc.vector.memset(inv[:, 1:2], 1.0)
+        nc.vector.memset(inv[:, 0:1], 1.0)
+        nc.vector.memset(inv[:, 1:2], -1.0)
         width = 2
         while width < HD:
             more = min(width, HD - width)
@@ -180,10 +180,11 @@ def tile_dbrxattention_pa_kernel(tc, x_words, x_scales, w_words, w_scales, out_q
             y = work.tile([P, 512], F32, name="y", bufs=8)
             nc.vector.tensor_tensor(out=a[:, :n], in0=acc, in1=cos_t[m][:, off : off + n], op=ALU.mult)
             nc.vector.tensor_tensor(
-                out=b[:, :n].rearrange("p (i t) -> p i t", t=2),
-                in0=acc.rearrange("p (i t) -> p i t", t=2)[:, :, ::-1],
-                in1=sin_t[m][:, off : off + n].rearrange("p (i t) -> p i t", t=2), op=ALU.mult)
-            nc.gpsimd.tensor_tensor(out=y[:, :n], in0=a[:, :n], in1=b[:, :n], op=ALU.add)
+                out=b[:, :n], in0=acc, in1=sin_t[m][:, off : off + n], op=ALU.mult)
+            nc.gpsimd.tensor_tensor(
+                out=y[:, :n].rearrange("p (i t) -> p i t", t=2),
+                in0=a[:, :n].rearrange("p (i t) -> p i t", t=2),
+                in1=b[:, :n].rearrange("p (i t) -> p i t", t=2)[:, :, ::-1], op=ALU.add)
             if which == "k" and c0 > 0 or turn[0] in GPSIMD_CLIPS:
                 nc.gpsimd.tensor_scalar(out=results[which][1][m][:, c0 : c0 + n], in0=y[:, :n], scalar1=CLAMP, scalar2=-CLAMP, op0=ALU.min, op1=ALU.max)
                 done(which, m, c0, c0 + n)
@@ -213,9 +214,10 @@ def tile_dbrxattention_pa_kernel(tc, x_words, x_scales, w_words, w_scales, out_q
                 advance(None)
             if b == 0:
                 accs = [psum.tile([P, 512], F32, name="acc") for m in range(M_TILES)]
-                for g in range(PASSES):
-                    for m in range(M_TILES):
-                        one_pass(accs[m][:, :n], m, c, n, g)
+                for pair in (0, 2):
+                    for g in range(PASSES):
+                        for m in (pair, pair + 1):
+                            one_pass(accs[m][:, :n], m, c, n, g)
                 for m in range(M_TILES):
                     finish(accs[m], m, c, n)
             else:

@@ -24,9 +24,9 @@ CLAMP = 8.0
 FLOPS = 2 * T * K * O
 BYTES = K * T // 2 + K * T // 32 + K * O // 2 + K * O // 32 + 4 * T * O
 
-LOADS = [(0, 512), (512, 512), (1024, 1024), (2048, 1024), (3072, 768)]
-BLOCKS = [(0, 512), (512, 512), (1024, 512), (1536, 512), (2048, 512), (2560, 512), (3072, 256), (3328, 512)]
-GPSIMD_CLIPS = (2, 6, 10, 14, 18, 22)
+LOADS = [(0, 512), (512, 512), (1024, 512), (1536, 1024), (2560, 1280)]
+UNITS = [[(0, 512)], [(512, 512), (1024, 512)], [(1536, 512), (2048, 512)], [(2560, 512), (3072, 256)], [(3328, 512)]]
+GPSIMD_CLIPS = (1, 3, 12, 13, 14, 15)
 REPEAT = 4
 TABLE = REPEAT * HD
 
@@ -39,7 +39,8 @@ def tile_dbrxattention_pa_kernel(tc, x_words, x_scales, w_words, w_scales, out_q
         psum = ctx.enter_context(tc.psum_pool(name="psum", bufs=8))
         ctx.enter_context(tc.manual_schedule())
 
-        xw = keep.tile([P, PASSES, 2 * T], U8, name="xw", align_bytes=64)
+        xw0 = keep.tile([P, PASSES, 2 * P], U8, name="xw0", align_bytes=64)
+        xw1 = keep.tile([P, PASSES, 2 * (T - P)], U8, name="xw1", align_bytes=64)
         xs = keep.tile([P, PASSES, T], U8, name="xs", align_bytes=64)
         ww = [keep.tile([P, PASSES, 2 * n], U8, name="ww%d" % i, align_bytes=64) for i, (c, n) in enumerate(LOADS)]
         ws = [keep.tile([P, PASSES, n], U8, name="ws%d" % i, align_bytes=64) for i, (c, n) in enumerate(LOADS)]
@@ -68,25 +69,21 @@ def tile_dbrxattention_pa_kernel(tc, x_words, x_scales, w_words, w_scales, out_q
             c, n = LOADS[i]
             return w_scales[:, :, c : c + n]
 
+        zero(nc.vector, xs)
+        zero(nc.gpsimd, ws[0])
         pos = keep.tile([P, M_TILES], F32, name="pos")
         nc.gpsimd.iota(pos[:], pattern=[[P, M_TILES]], base=0, channel_multiplier=1,
                        allow_small_or_imprecise_dtypes=True)
-        zero(nc.vector, xs)
-        zero(nc.vector, ws[0])
-        for i in range(1, len(LOADS)):
-            zero(nc.gpsimd, ws[i])
+        zero(nc.gpsimd, ws[1])
 
-        load_words(xw, x_words, 0, 1)
-        load_words(ww[0], w_cols(0), 0, 1)
+        load_words(xw0, x_words[:, :, 0 : 2 * P], 0, PASSES)
+        load_words(ww[0], w_cols(0), 0, 2)
         load_scales(xs, x_scales)
         load_scales(ws[0], s_cols(0))
-        load_words(xw, x_words, 1, 3)
-        load_words(ww[0], w_cols(0), 1, 3)
-        load_words(xw, x_words, 3, 5)
-        load_words(ww[0], w_cols(0), 3, 5)
-        for i in range(1, len(LOADS)):
-            load_words(ww[i], w_cols(i), 0, PASSES)
-            load_scales(ws[i], s_cols(i))
+        load_words(ww[0], w_cols(0), 2, PASSES)
+        load_words(xw1, x_words[:, :, 2 * P :], 0, PASSES)
+        load_words(ww[1], w_cols(1), 0, PASSES)
+        load_scales(ws[1], s_cols(1))
 
         ratio = ROPE_BASE ** (-2.0 / HD)
         inv = keep.tile([P, HD], F32, name="inv")
@@ -106,9 +103,10 @@ def tile_dbrxattention_pa_kernel(tc, x_words, x_scales, w_words, w_scales, out_q
             turns = keep.tile([P, 2, count, HD], F32, name="turns" + name)
             whole = keep.tile([P, 2, count, HD], I32, name="whole" + name)
             for m in range(m0, m1):
-                nc.vector.tensor_scalar(out=turns[:, 0, m - m0, :], in0=inv[:], scalar1=pos[:, m : m + 1],
+                nc.gpsimd.tensor_scalar(out=turns[:, 0, m - m0, :], in0=inv[:], scalar1=pos[:, m : m + 1],
                                         scalar2=1.0 / (2.0 * math.pi), op0=ALU.mult, op1=ALU.mult)
-            nc.vector.tensor_scalar_add(turns[:, 1, :, :], turns[:, 0, :, :], 0.25)
+            nc.gpsimd.tensor_scalar(out=turns[:, 1, :, :], in0=turns[:, 0, :, :], scalar1=1.0, scalar2=0.25,
+                                    op0=ALU.mult, op1=ALU.add)
             nc.vector.tensor_copy(out=whole[:], in_=turns[:])
             nc.vector.tensor_tensor(out=turns[:], in0=turns[:], in1=whole[:], op=ALU.subtract)
             for m in range(m0, m1):
@@ -120,6 +118,10 @@ def tile_dbrxattention_pa_kernel(tc, x_words, x_scales, w_words, w_scales, out_q
 
         angles(0, 1, "a")
         angles(1, M_TILES, "b")
+        for i in range(2, len(LOADS)):
+            zero(nc.gpsimd, ws[i])
+            load_words(ww[i], w_cols(i), 0, PASSES)
+            load_scales(ws[i], s_cols(i))
 
         res_q = [keep.tile([P, D], F32, name="q%d" % m) for m in range(M_TILES)]
         res_k = [keep.tile([P, KVD], F32, name="k%d" % m) for m in range(M_TILES)]
@@ -130,7 +132,7 @@ def tile_dbrxattention_pa_kernel(tc, x_words, x_scales, w_words, w_scales, out_q
             at = c - LOADS[i][0]
             nc.tensor.matmul_mx(
                 out=acc,
-                lhsT=xw[:, g, 2 * P * m : 2 * P * (m + 1)].bitcast(FP4X4),
+                lhsT=(xw0[:, g, :] if m == 0 else xw1[:, g, 2 * P * (m - 1) : 2 * P * m]).bitcast(FP4X4),
                 lhsT_scale=xs[:, g, P * m : P * (m + 1)],
                 rhs=ww[i][:, g, 2 * at : 2 * (at + n)].bitcast(FP4X4),
                 rhs_scale=ws[i][:, g, at : at + n],
@@ -138,6 +140,7 @@ def tile_dbrxattention_pa_kernel(tc, x_words, x_scales, w_words, w_scales, out_q
 
         turn = [0]
         chain = []
+        late = []
         ready = {}
         stored = {}
         results = {"q": (out_q, res_q), "k": (out_k, res_k), "v": (out_v, res_v)}
@@ -150,6 +153,9 @@ def tile_dbrxattention_pa_kernel(tc, x_words, x_scales, w_words, w_scales, out_q
             if h1 > h0:
                 stored[key] = h1
                 dram, res = results[which]
+                if which == "k":
+                    late.append(m)
+                    return
                 nc.sync.dma_start(
                     out=dram[0, h0:h1, P * m : P * (m + 1), :].rearrange("h p d -> p h d"),
                     in_=res[m][:, HD * h0 : HD * h1].rearrange("p (h d) -> p h d", d=HD))
@@ -173,56 +179,67 @@ def tile_dbrxattention_pa_kernel(tc, x_words, x_scales, w_words, w_scales, out_q
             while chain and chain[0][0] == 3:
                 chain.pop(0)
 
-        def rope(acc, m, c, n, which, c0):
-            off = c % HD
-            a = work.tile([P, 512], F32, name="a")
-            b = work.tile([P, 512], F32, name="b")
-            y = work.tile([P, 512], F32, name="y", bufs=8)
-            nc.vector.tensor_tensor(out=a[:, :n], in0=acc, in1=cos_t[m][:, off : off + n], op=ALU.mult)
-            nc.vector.tensor_tensor(
-                out=b[:, :n], in0=acc, in1=sin_t[m][:, off : off + n], op=ALU.mult)
+        def rope_unit(parts, m, which, c0):
+            width = sum(n for acc, c, n in parts)
+            a = work.tile([P, 1024], F32, name="a", bufs=3)
+            b = work.tile([P, 1024], F32, name="b", bufs=3)
+            y = work.tile([P, 1024], F32, name="y", bufs=4)
+            at = 0
+            for acc, c, n in parts:
+                off = c % HD
+                nc.vector.tensor_tensor(out=a[:, at : at + n], in0=acc, in1=cos_t[m][:, off : off + n], op=ALU.mult)
+                nc.vector.tensor_tensor(out=b[:, at : at + n], in0=acc, in1=sin_t[m][:, off : off + n], op=ALU.mult)
+                at += n
             nc.gpsimd.tensor_tensor(
-                out=y[:, :n].rearrange("p (i t) -> p i t", t=2),
-                in0=a[:, :n].rearrange("p (i t) -> p i t", t=2),
-                in1=b[:, :n].rearrange("p (i t) -> p i t", t=2)[:, :, ::-1], op=ALU.add)
-            if which == "k" and c0 > 0 or turn[0] in GPSIMD_CLIPS:
-                nc.gpsimd.tensor_scalar(out=results[which][1][m][:, c0 : c0 + n], in0=y[:, :n], scalar1=CLAMP, scalar2=-CLAMP, op0=ALU.min, op1=ALU.max)
-                done(which, m, c0, c0 + n)
+                out=y[:, :width].rearrange("p (i t) -> p i t", t=2),
+                in0=a[:, :width].rearrange("p (i t) -> p i t", t=2),
+                in1=b[:, :width].rearrange("p (i t) -> p i t", t=2)[:, :, ::-1], op=ALU.add)
+            if turn[0] in GPSIMD_CLIPS:
+                nc.gpsimd.tensor_scalar(out=results[which][1][m][:, c0 : c0 + width], in0=y[:, :width], scalar1=CLAMP, scalar2=-CLAMP, op0=ALU.min, op1=ALU.max)
+                done(which, m, c0, c0 + width)
             else:
-                advance([0, y, n, which, m, c0])
+                advance([0, y, width, which, m, c0])
             turn[0] += 1
 
-        def finish(acc, m, c, n):
-            if c < D:
-                rope(acc[:, :n], m, c, n, "q", c)
-                return
-            kn = max(0, min(n, D + KVD - c))
-            if kn:
-                rope(acc[:, :kn], m, c, kn, "k", c - D)
-            if kn < n:
-                if kn == 0:
-                    advance(None)
-                v0 = c + kn - D - KVD
-                v1 = c + n - D - KVD
-                nc.vector.tensor_scalar(out=res_v[m][:, v0:v1], in0=acc[:, kn:n], scalar1=CLAMP, scalar2=-CLAMP,
-                                        op0=ALU.min, op1=ALU.max)
-                done("v", m, v0, v1)
+        def clip_v(acc, m, v0, v1):
+            nc.vector.tensor_scalar(out=res_v[m][:, v0:v1], in0=acc, scalar1=CLAMP, scalar2=-CLAMP,
+                                    op0=ALU.min, op1=ALU.max)
+            done("v", m, v0, v1)
 
-        for b, (c, n) in enumerate(BLOCKS):
-            if c == D + 512:
+        def finish(accs, m, unit):
+            c = unit[0][0]
+            if c < D:
+                rope_unit([(acc[:, :n], c, n) for acc, (c, n) in zip(accs, unit)], m, "q", c)
+            elif c < D + KVD:
+                split = D + KVD - unit[1][0]
+                rope_unit([(accs[0][:, :512], c, 512), (accs[1][:, :split], unit[1][0], split)], m, "k", 0)
+                clip_v(accs[1][:, split : unit[1][1]], m, 0, unit[1][1] - split)
+                advance(None)
+            else:
+                clip_v(accs[0][:, :512], m, c - D - KVD, c - D - KVD + 512)
+
+        for u, unit in enumerate(UNITS):
+            if u == len(UNITS) - 1:
                 advance(None)
                 advance(None)
-            if b == 0:
+                for m in late:
+                    nc.scalar.dma_start(
+                        out=out_k[0, :, P * m : P * (m + 1), :].rearrange("h p d -> p h d"),
+                        in_=res_k[m][:].rearrange("p (h d) -> p h d", d=HD))
+            if u == 0:
+                c, n = unit[0]
                 accs = [psum.tile([P, 512], F32, name="acc") for m in range(M_TILES)]
-                for pair in (0, 2):
-                    for g in range(PASSES):
-                        for m in (pair, pair + 1):
-                            one_pass(accs[m][:, :n], m, c, n, g)
                 for m in range(M_TILES):
-                    finish(accs[m], m, c, n)
+                    for g in range(PASSES):
+                        one_pass(accs[m][:, :n], m, c, n, g)
+                for m in range(M_TILES):
+                    finish([accs[m]], m, unit)
             else:
                 for m in range(M_TILES):
-                    acc = psum.tile([P, 512], F32, name="acc")
-                    for g in range(PASSES):
-                        one_pass(acc[:, :n], m, c, n, g)
-                    finish(acc, m, c, n)
+                    accs = []
+                    for c, n in unit:
+                        acc = psum.tile([P, 512], F32, name="acc")
+                        for g in range(PASSES):
+                            one_pass(acc[:, :n], m, c, n, g)
+                        accs.append(acc)
+                    finish(accs, m, unit)

@@ -45,8 +45,8 @@ def tile_dbrxattention_pa_kernel(tc, x_words, x_scales, w_words, w_scales, out_q
         ww = [keep.tile([P, PASSES, 2 * n], U8, name="ww%d" % i, align_bytes=64) for i, (c, n) in enumerate(LOADS)]
         ws = [keep.tile([P, PASSES, n], U8, name="ws%d" % i, align_bytes=64) for i, (c, n) in enumerate(LOADS)]
 
-        def zero(engine, plane):
-            engine.memset(plane[:].rearrange("p g n -> p (g n)").bitcast(I32), 0)
+        def zero(engine, plane, g0=0, g1=PASSES):
+            engine.memset(plane[:, g0:g1, :].rearrange("p g n -> p (g n)").bitcast(I32), 0)
 
         def load_words(dst, src, g0, g1):
             nc.sync.dma_start(
@@ -74,7 +74,6 @@ def tile_dbrxattention_pa_kernel(tc, x_words, x_scales, w_words, w_scales, out_q
         pos = keep.tile([P, M_TILES], F32, name="pos")
         nc.gpsimd.iota(pos[:], pattern=[[P, M_TILES]], base=0, channel_multiplier=1,
                        allow_small_or_imprecise_dtypes=True)
-        zero(nc.gpsimd, ws[1])
 
         load_words(xw0, x_words[:, :, 0 : 2 * P], 0, PASSES)
         load_words(ww[0], w_cols(0), 0, 2)
@@ -82,46 +81,60 @@ def tile_dbrxattention_pa_kernel(tc, x_words, x_scales, w_words, w_scales, out_q
         load_scales(ws[0], s_cols(0))
         load_words(ww[0], w_cols(0), 2, PASSES)
         load_words(xw1, x_words[:, :, 2 * P :], 0, PASSES)
-        load_words(ww[1], w_cols(1), 0, PASSES)
-        load_scales(ws[1], s_cols(1))
-
         ratio = ROPE_BASE ** (-2.0 / HD)
         inv = keep.tile([P, HD], F32, name="inv")
         nc.vector.memset(inv[:, 0:1], 1.0)
         nc.vector.memset(inv[:, 1:2], -1.0)
+        fillers = [(1, 0, 5), (2, 0, 5), (3, 0, 3), (3, 3, 5), (4, 0, 3), (4, 3, 5)]
         width = 2
         while width < HD:
             more = min(width, HD - width)
             nc.vector.tensor_scalar_mul(inv[:, width : width + more], inv[:, 0:more], ratio ** (width // 2))
             width += more
+            if fillers:
+                i, g0, g1 = fillers.pop(0)
+                zero(nc.vector, ws[i], g0, g1)
+        for i in range(1, len(LOADS)):
+            load_words(ww[i], w_cols(i), 0, PASSES)
+            load_scales(ws[i], s_cols(i))
 
         sin_t = [keep.tile([P, TABLE], F32, name="sin%d" % m) for m in range(M_TILES)]
         cos_t = [keep.tile([P, TABLE], F32, name="cos%d" % m) for m in range(M_TILES)]
+        turns_a = keep.tile([P, 2, 1, HD], F32, name="turns_a")
+        whole_a = keep.tile([P, 2, 1, HD], I32, name="whole_a")
+        turns_b = keep.tile([P, 2, M_TILES - 1, HD], F32, name="turns_b")
+        whole_b = keep.tile([P, 2, M_TILES - 1, HD], I32, name="whole_b")
 
-        def angles(m0, m1, name):
-            count = m1 - m0
-            turns = keep.tile([P, 2, count, HD], F32, name="turns" + name)
-            whole = keep.tile([P, 2, count, HD], I32, name="whole" + name)
-            for m in range(m0, m1):
-                nc.gpsimd.tensor_scalar(out=turns[:, 0, m - m0, :], in0=inv[:], scalar1=pos[:, m : m + 1],
-                                        scalar2=1.0 / (2.0 * math.pi), op0=ALU.mult, op1=ALU.mult)
-            nc.gpsimd.tensor_scalar(out=turns[:, 1, :, :], in0=turns[:, 0, :, :], scalar1=1.0, scalar2=0.25,
-                                    op0=ALU.mult, op1=ALU.add)
-            nc.vector.tensor_copy(out=whole[:], in_=turns[:])
+        def sine_turns(dst, m):
+            nc.vector.tensor_scalar(out=dst, in0=inv[:], scalar1=pos[:, m : m + 1],
+                                    scalar2=1.0 / (2.0 * math.pi), op0=ALU.mult, op1=ALU.mult)
+
+        def cosine_turns(turns):
+            nc.vector.tensor_scalar_add(turns[:, 1, :, :], turns[:, 0, :, :], 0.25)
+
+        def subtract_whole(turns, whole):
             nc.vector.tensor_tensor(out=turns[:], in0=turns[:], in1=whole[:], op=ALU.subtract)
-            for m in range(m0, m1):
-                for kind, table in ((1, cos_t[m]), (0, sin_t[m])):
-                    nc.scalar.activation(
-                        out=table[:].rearrange("p (h d) -> p h d", d=HD),
-                        in_=turns[:, kind, m - m0 : m - m0 + 1, :].to_broadcast([P, REPEAT, HD]),
-                        func=ACT.Sin, scale=2.0 * math.pi)
 
-        angles(0, 1, "a")
-        angles(1, M_TILES, "b")
-        for i in range(2, len(LOADS)):
-            zero(nc.gpsimd, ws[i])
-            load_words(ww[i], w_cols(i), 0, PASSES)
-            load_scales(ws[i], s_cols(i))
+        def tables(turns, at, m):
+            for kind, table in ((1, cos_t[m]), (0, sin_t[m])):
+                nc.scalar.activation(
+                    out=table[:].rearrange("p (h d) -> p h d", d=HD),
+                    in_=turns[:, kind, at : at + 1, :].to_broadcast([P, REPEAT, HD]),
+                    func=ACT.Sin, scale=2.0 * math.pi)
+
+        sine_turns(turns_a[:, 0, 0, :], 0)
+        sine_turns(turns_b[:, 0, 0, :], 1)
+        cosine_turns(turns_a)
+        sine_turns(turns_b[:, 0, 1, :], 2)
+        nc.vector.tensor_copy(out=whole_a[:], in_=turns_a[:])
+        sine_turns(turns_b[:, 0, 2, :], 3)
+        subtract_whole(turns_a, whole_a)
+        tables(turns_a, 0, 0)
+        cosine_turns(turns_b)
+        nc.vector.tensor_copy(out=whole_b[:], in_=turns_b[:])
+        subtract_whole(turns_b, whole_b)
+        for m in range(1, M_TILES):
+            tables(turns_b, m - 1, m)
 
         res_q = [keep.tile([P, D], F32, name="q%d" % m) for m in range(M_TILES)]
         res_k = [keep.tile([P, KVD], F32, name="k%d" % m) for m in range(M_TILES)]
@@ -139,7 +152,6 @@ def tile_dbrxattention_pa_kernel(tc, x_words, x_scales, w_words, w_scales, out_q
                 start=(g == 0), stop=(g == PASSES - 1))
 
         turn = [0]
-        chain = []
         late = []
         ready = {}
         stored = {}
@@ -160,24 +172,16 @@ def tile_dbrxattention_pa_kernel(tc, x_words, x_scales, w_words, w_scales, out_q
                     out=dram[0, h0:h1, P * m : P * (m + 1), :].rearrange("h p d -> p h d"),
                     in_=res[m][:, HD * h0 : HD * h1].rearrange("p (h d) -> p h d", d=HD))
 
-        def step_chain(entry):
-            step, y, n, which, m, c0 = entry
-            if step == 0:
-                nc.scalar.activation(out=y[:, :n], in_=y[:, :n], func=ACT.Relu, scale=-1.0, bias=CLAMP)
-            elif step == 1:
-                nc.scalar.activation(out=y[:, :n], in_=y[:, :n], func=ACT.Relu, scale=-1.0, bias=2.0 * CLAMP)
-            else:
-                nc.scalar.activation(out=results[which][1][m][:, c0 : c0 + n], in_=y[:, :n], func=ACT.Identity, bias=-CLAMP)
-                done(which, m, c0, c0 + n)
-            entry[0] = step + 1
-
-        def advance(entry):
-            if entry is not None:
-                chain.append(entry)
-            for e in list(chain):
-                step_chain(e)
-            while chain and chain[0][0] == 3:
-                chain.pop(0)
+        def scalar_clip(y, width, which, m, c0):
+            cut = 512 if width > 512 else width // 2
+            halves = [(0, cut), (cut, width)]
+            for i, j in halves:
+                nc.scalar.activation(out=y[:, i:j], in_=y[:, i:j], func=ACT.Relu, scale=-1.0, bias=CLAMP)
+            for i, j in halves:
+                nc.scalar.activation(out=y[:, i:j], in_=y[:, i:j], func=ACT.Relu, scale=-1.0, bias=2.0 * CLAMP)
+            for i, j in halves:
+                nc.scalar.activation(out=results[which][1][m][:, c0 + i : c0 + j], in_=y[:, i:j], func=ACT.Identity, bias=-CLAMP)
+                done(which, m, c0 + i, c0 + j)
 
         def rope_unit(parts, m, which, c0):
             width = sum(n for acc, c, n in parts)
@@ -198,7 +202,7 @@ def tile_dbrxattention_pa_kernel(tc, x_words, x_scales, w_words, w_scales, out_q
                 nc.gpsimd.tensor_scalar(out=results[which][1][m][:, c0 : c0 + width], in0=y[:, :width], scalar1=CLAMP, scalar2=-CLAMP, op0=ALU.min, op1=ALU.max)
                 done(which, m, c0, c0 + width)
             else:
-                advance([0, y, width, which, m, c0])
+                scalar_clip(y, width, which, m, c0)
             turn[0] += 1
 
         def clip_v(acc, m, v0, v1):
@@ -214,14 +218,12 @@ def tile_dbrxattention_pa_kernel(tc, x_words, x_scales, w_words, w_scales, out_q
                 split = D + KVD - unit[1][0]
                 rope_unit([(accs[0][:, :512], c, 512), (accs[1][:, :split], unit[1][0], split)], m, "k", 0)
                 clip_v(accs[1][:, split : unit[1][1]], m, 0, unit[1][1] - split)
-                advance(None)
             else:
-                clip_v(accs[0][:, :512], m, c - D - KVD, c - D - KVD + 512)
+                for acc, (c, n) in zip(accs, unit):
+                    clip_v(acc[:, :n], m, c - D - KVD, c - D - KVD + n)
 
         for u, unit in enumerate(UNITS):
             if u == len(UNITS) - 1:
-                advance(None)
-                advance(None)
                 for m in late:
                     nc.scalar.dma_start(
                         out=out_k[0, :, P * m : P * (m + 1), :].rearrange("h p d -> p h d"),
@@ -236,6 +238,8 @@ def tile_dbrxattention_pa_kernel(tc, x_words, x_scales, w_words, w_scales, out_q
                     finish([accs[m]], m, unit)
             else:
                 for m in range(M_TILES):
+                    if u == len(UNITS) - 1 and m == M_TILES - 1:
+                        unit = [(3328, 256), (3584, 256)]
                     accs = []
                     for c, n in unit:
                         acc = psum.tile([P, 512], F32, name="acc")

import math
from contextlib import ExitStack

import concourse.mybir as mybir

F32 = mybir.dt.float32
I32 = mybir.dt.int32
U8 = mybir.dt.uint8
FP4X4 = mybir.dt.float4_e2m1fn_x4
ALU = mybir.AluOpType
ACT = mybir.ActivationFunctionType

P = 128
T, H, KV, HD = 512, 16, 4, 160
D = H * HD
KVD = KV * HD
O = D + 2 * KVD
K = D
PASSES = K // 512
M_TILES = T // P
ROPE_BASE = 500000.0
CLAMP = 8.0

FLOPS = 2 * T * K * O
BYTES = K * T // 2 + K * T // 32 + K * O // 2 + K * O // 32 + 4 * T * O

LOADS = [(0, 512), (512, 512), (1024, 512), (1536, 1024), (2560, 1280)]
UNITS = [[(0, 512)], [(512, 512), (1024, 512)], [(1536, 512), (2048, 512)], [(2560, 512), (3072, 256)], [(3328, 512)]]
GPSIMD_CLIPS = (1, 3, 12, 13, 14, 15)
REPEAT = 4
TABLE = REPEAT * HD


def tile_dbrxattention_pa_kernel(tc, x_words, x_scales, w_words, w_scales, out_q, out_k, out_v):
    nc = tc.nc
    with ExitStack() as ctx:
        keep = ctx.enter_context(tc.tile_pool(name="keep", bufs=1))
        work = ctx.enter_context(tc.tile_pool(name="work", bufs=4))
        psum = ctx.enter_context(tc.psum_pool(name="psum", bufs=8))
        ctx.enter_context(tc.manual_schedule())

        xw0 = keep.tile([P, PASSES, 2 * P], U8, name="xw0", align_bytes=64)
        xw1 = keep.tile([P, PASSES, 2 * (T - P)], U8, name="xw1", align_bytes=64)
        xs = keep.tile([P, PASSES, T], U8, name="xs", align_bytes=64)
        ww = [keep.tile([P, PASSES, 2 * n], U8, name="ww%d" % i, align_bytes=64) for i, (c, n) in enumerate(LOADS)]
        ws = [keep.tile([P, PASSES, n], U8, name="ws%d" % i, align_bytes=64) for i, (c, n) in enumerate(LOADS)]

        def zero(engine, plane, g0=0, g1=PASSES):
            engine.memset(plane[:, g0:g1, :].rearrange("p g n -> p (g n)").bitcast(I32), 0)

        def load_words(dst, src, g0, g1):
            nc.sync.dma_start(
                out=dst[:, g0:g1, :].bitcast(I32),
                in_=src[g0:g1].rearrange("g p n -> p g n").bitcast(I32),
            )

        def load_scales(dst, src):
            for quad in range(4):
                nc.sync.dma_start(
                    out=dst[32 * quad : 32 * quad + 4, :, :].bitcast(I32),
                    in_=src[:, 4 * quad : 4 * quad + 4, :].rearrange("g r n -> r g n").bitcast(I32),
                )

        def w_cols(i):
            c, n = LOADS[i]
            return w_words[:, :, 2 * c : 2 * (c + n)]

        def s_cols(i):
            c, n = LOADS[i]
            return w_scales[:, :, c : c + n]

        zero(nc.vector, xs)
        zero(nc.gpsimd, ws[0])
        pos = keep.tile([P, M_TILES], F32, name="pos")
        nc.gpsimd.iota(pos[:], pattern=[[P, M_TILES]], base=0, channel_multiplier=1,
                       allow_small_or_imprecise_dtypes=True)

        load_words(xw0, x_words[:, :, 0 : 2 * P], 0, PASSES)
        load_words(ww[0], w_cols(0), 0, 2)
        load_scales(xs, x_scales)
        load_scales(ws[0], s_cols(0))
        load_words(ww[0], w_cols(0), 2, PASSES)
        load_words(xw1, x_words[:, :, 2 * P :], 0, PASSES)
        ratio = ROPE_BASE ** (-2.0 / HD)
        inv = keep.tile([P, HD], F32, name="inv")
        nc.vector.memset(inv[:, 0:1], 1.0)
        nc.vector.memset(inv[:, 1:2], -1.0)
        fillers = [(1, 0, 5), (2, 0, 5), (3, 0, 3), (3, 3, 5), (4, 0, 3), (4, 3, 5)]
        width = 2
        while width < HD:
            more = min(width, HD - width)
            nc.vector.tensor_scalar_mul(inv[:, width : width + more], inv[:, 0:more], ratio ** (width // 2))
            width += more
            if fillers:
                i, g0, g1 = fillers.pop(0)
                zero(nc.vector, ws[i], g0, g1)
        for i in range(1, len(LOADS)):
            load_words(ww[i], w_cols(i), 0, PASSES)
            load_scales(ws[i], s_cols(i))

        sin_t = [keep.tile([P, TABLE], F32, name="sin%d" % m) for m in range(M_TILES)]
        cos_t = [keep.tile([P, TABLE], F32, name="cos%d" % m) for m in range(M_TILES)]
        turns_a = keep.tile([P, 2, 1, HD], F32, name="turns_a")
        whole_a = keep.tile([P, 2, 1, HD], I32, name="whole_a")
        turns_b = keep.tile([P, 2, M_TILES - 1, HD], F32, name="turns_b")
        whole_b = keep.tile([P, 2, M_TILES - 1, HD], I32, name="whole_b")

        def sine_turns(dst, m):
            nc.vector.tensor_scalar(out=dst, in0=inv[:], scalar1=pos[:, m : m + 1],
                                    scalar2=1.0 / (2.0 * math.pi), op0=ALU.mult, op1=ALU.mult)

        def cosine_turns(turns):
            nc.vector.tensor_scalar_add(turns[:, 1, :, :], turns[:, 0, :, :], 0.25)

        def subtract_whole(turns, whole):
            nc.vector.tensor_tensor(out=turns[:], in0=turns[:], in1=whole[:], op=ALU.subtract)

        def tables(turns, at, m):
            for kind, table in ((1, cos_t[m]), (0, sin_t[m])):
                nc.scalar.activation(
                    out=table[:].rearrange("p (h d) -> p h d", d=HD),
                    in_=turns[:, kind, at : at + 1, :].to_broadcast([P, REPEAT, HD]),
                    func=ACT.Sin, scale=2.0 * math.pi)

        sine_turns(turns_a[:, 0, 0, :], 0)
        sine_turns(turns_b[:, 0, 0, :], 1)
        cosine_turns(turns_a)
        sine_turns(turns_b[:, 0, 1, :], 2)
        nc.vector.tensor_copy(out=whole_a[:], in_=turns_a[:])
        sine_turns(turns_b[:, 0, 2, :], 3)
        subtract_whole(turns_a, whole_a)
        tables(turns_a, 0, 0)
        cosine_turns(turns_b)
        nc.vector.tensor_copy(out=whole_b[:], in_=turns_b[:])
        subtract_whole(turns_b, whole_b)
        for m in range(1, M_TILES):
            tables(turns_b, m - 1, m)

        res_q = [keep.tile([P, D], F32, name="q%d" % m) for m in range(M_TILES)]
        res_k = [keep.tile([P, KVD], F32, name="k%d" % m) for m in range(M_TILES)]
        res_v = [keep.tile([P, KVD], F32, name="v%d" % m) for m in range(M_TILES)]

        def one_pass(acc, m, c, n, g):
            i = max(j for j in range(len(LOADS)) if LOADS[j][0] <= c)
            at = c - LOADS[i][0]
            nc.tensor.matmul_mx(
                out=acc,
                lhsT=(xw0[:, g, :] if m == 0 else xw1[:, g, 2 * P * (m - 1) : 2 * P * m]).bitcast(FP4X4),
                lhsT_scale=xs[:, g, P * m : P * (m + 1)],
                rhs=ww[i][:, g, 2 * at : 2 * (at + n)].bitcast(FP4X4),
                rhs_scale=ws[i][:, g, at : at + n],
                start=(g == 0), stop=(g == PASSES - 1))

        turn = [0]
        late = []
        ready = {}
        stored = {}
        results = {"q": (out_q, res_q), "k": (out_k, res_k), "v": (out_v, res_v)}

        def done(which, m, c0, c1):
            key = (which, m)
            assert ready.get(key, 0) == c0
            ready[key] = c1
            h0, h1 = stored.get(key, 0), c1 // HD
            if h1 > h0:
                stored[key] = h1
                dram, res = results[which]
                if which == "k":
                    late.append(m)
                    return
                nc.sync.dma_start(
                    out=dram[0, h0:h1, P * m : P * (m + 1), :].rearrange("h p d -> p h d"),
                    in_=res[m][:, HD * h0 : HD * h1].rearrange("p (h d) -> p h d", d=HD))

        def scalar_clip(y, width, which, m, c0):
            cut = 512 if width > 512 else width // 2
            halves = [(0, cut), (cut, width)]
            for i, j in halves:
                nc.scalar.activation(out=y[:, i:j], in_=y[:, i:j], func=ACT.Relu, scale=-1.0, bias=CLAMP)
            for i, j in halves:
                nc.scalar.activation(out=y[:, i:j], in_=y[:, i:j], func=ACT.Relu, scale=-1.0, bias=2.0 * CLAMP)
            for i, j in halves:
                nc.scalar.activation(out=results[which][1][m][:, c0 + i : c0 + j], in_=y[:, i:j], func=ACT.Identity, bias=-CLAMP)
                done(which, m, c0 + i, c0 + j)

        def rope_unit(parts, m, which, c0):
            width = sum(n for acc, c, n in parts)
            a = work.tile([P, 1024], F32, name="a", bufs=3)
            b = work.tile([P, 1024], F32, name="b", bufs=3)
            y = work.tile([P, 1024], F32, name="y", bufs=4)
            at = 0
            for acc, c, n in parts:
                off = c % HD
                nc.vector.tensor_tensor(out=a[:, at : at + n], in0=acc, in1=cos_t[m][:, off : off + n], op=ALU.mult)
                nc.vector.tensor_tensor(out=b[:, at : at + n], in0=acc, in1=sin_t[m][:, off : off + n], op=ALU.mult)
                at += n
            nc.gpsimd.tensor_tensor(
                out=y[:, :width].rearrange("p (i t) -> p i t", t=2),
                in0=a[:, :width].rearrange("p (i t) -> p i t", t=2),
                in1=b[:, :width].rearrange("p (i t) -> p i t", t=2)[:, :, ::-1], op=ALU.add)
            if turn[0] in GPSIMD_CLIPS:
                nc.gpsimd.tensor_scalar(out=results[which][1][m][:, c0 : c0 + width], in0=y[:, :width], scalar1=CLAMP, scalar2=-CLAMP, op0=ALU.min, op1=ALU.max)
                done(which, m, c0, c0 + width)
            else:
                scalar_clip(y, width, which, m, c0)
            turn[0] += 1

        def clip_v(acc, m, v0, v1):
            nc.vector.tensor_scalar(out=res_v[m][:, v0:v1], in0=acc, scalar1=CLAMP, scalar2=-CLAMP,
                                    op0=ALU.min, op1=ALU.max)
            done("v", m, v0, v1)

        def finish(accs, m, unit):
            c = unit[0][0]
            if c < D:
                rope_unit([(acc[:, :n], c, n) for acc, (c, n) in zip(accs, unit)], m, "q", c)
            elif c < D + KVD:
                split = D + KVD - unit[1][0]
                rope_unit([(accs[0][:, :512], c, 512), (accs[1][:, :split], unit[1][0], split)], m, "k", 0)
                clip_v(accs[1][:, split : unit[1][1]], m, 0, unit[1][1] - split)
            else:
                for acc, (c, n) in zip(accs, unit):
                    clip_v(acc[:, :n], m, c - D - KVD, c - D - KVD + n)

        for u, unit in enumerate(UNITS):
            if u == len(UNITS) - 1:
                for m in late:
                    nc.scalar.dma_start(
                        out=out_k[0, :, P * m : P * (m + 1), :].rearrange("h p d -> p h d"),
                        in_=res_k[m][:].rearrange("p (h d) -> p h d", d=HD))
            if u == 0:
                c, n = unit[0]
                accs = [psum.tile([P, 512], F32, name="acc") for m in range(M_TILES)]
                for m in range(M_TILES):
                    for g in range(PASSES):
                        one_pass(accs[m][:, :n], m, c, n, g)
                for m in range(M_TILES):
                    finish([accs[m]], m, unit)
            else:
                for m in range(M_TILES):
                    if u == len(UNITS) - 1 and m == M_TILES - 1:
                        unit = [(3328, 256), (3584, 256)]
                    accs = []
                    for c, n in unit:
                        acc = psum.tile([P, 512], F32, name="acc")
                        for g in range(PASSES):
                            one_pass(acc[:, :n], m, c, n, g)
                        accs.append(acc)
                    finish(accs, m, unit)
